import numpy as np
import ml_dtypes


def mxq(x, axis, fmt="e4m3"):
    dtype, down = {"e4m3": (ml_dtypes.float8_e4m3fn, 7), "e5m2": (ml_dtypes.float8_e5m2, 14)}[fmt]
    v = np.moveaxis(np.asarray(x, np.float32).astype(ml_dtypes.bfloat16).astype(np.float64), axis, -1)
    blocks = v.reshape(v.shape[:-1] + (-1, 32))
    amax = np.abs(blocks).max(-1, keepdims=True)
    byte = np.maximum(np.where(amax > 0, np.frexp(amax)[1] - 1 + 127, 0) - down, 1)
    scale = np.exp2(byte - 127.0)
    codes = (blocks / scale).astype(np.float32).astype(dtype).astype(np.float64)
    return np.moveaxis((codes * scale).reshape(v.shape), -1, axis)


WIDE = False


def mx_kscale(k):
    if not WIDE:
        return np.ones(k)
    levels = np.array([10, -10, 5, -5, 0])
    if k % 512:
        return np.exp2(np.random.permutation(np.resize(levels, k // 32))).repeat(32)
    a = np.empty((k // 512, 16))
    for p in range(k // 512):
        a[p, :8] = np.random.permutation(np.resize(levels, 8))
        for g in range(8):
            far = levels[np.abs(levels - a[p, g]) >= 10]
            a[p, g + 8] = far[np.random.randint(len(far))]
    return np.exp2(a.ravel()).repeat(32)


BF16 = ml_dtypes.bfloat16


def bf(x):
    return np.asarray(x, np.float32).astype(BF16)


def f64(x):
    return np.asarray(x).astype(np.float64)


B, S, DIM, H, NOPE, ROPE, VHD, KV_RANK = 4, 2048, 512, 2, 128, 64, 128, 512
QKHD = NOPE + ROPE
HALF = ROPE // 2
EPS = 1e-5


def rope(u, cos, sin):
    ur = u.reshape(u.shape[:-1] + (HALF, 2))
    a, b = ur[..., 0], ur[..., 1]
    c = cos[None, :, None, :]
    s = sin[None, :, None, :]
    return np.stack([a * c - b * s, a * s + b * c], axis=-1).reshape(u.shape)


def draw0():
    s = mx_kscale(DIM)
    t = mx_kscale(KV_RANK)
    inv_freq = 1.0 / 10000.0 ** (np.arange(0, ROPE, 2) / ROPE)
    ang = np.arange(S)[:, None] * inv_freq[None, :]
    return {"x": bf(np.random.standard_normal((B, S, DIM)) * s),
            "wkv_a_w": bf(np.random.standard_normal((DIM, KV_RANK + H * ROPE)) / np.sqrt(DIM) / s[:, None]),
            "wkv_a_b": bf(np.random.standard_normal(KV_RANK + H * ROPE) * 0.2),
            "kvn_g": bf((1.0 + 0.1 * np.random.standard_normal(KV_RANK)) * t),
            "kvn_b": bf(0.1 * np.random.standard_normal(KV_RANK) * t),
            "wk_w": bf(np.random.standard_normal((KV_RANK, H * NOPE)) / np.sqrt(KV_RANK) / t[:, None]),
            "wk_b": bf(np.random.standard_normal(H * NOPE) * 0.2),
            "wv_w": bf(np.random.standard_normal((KV_RANK, H * VHD)) / np.sqrt(KV_RANK) / t[:, None]),
            "wv_b": bf(np.random.standard_normal(H * VHD) * 0.2),
            "cos": bf(np.cos(ang)), "sin": bf(np.sin(ang))}


def core(x, wkv_a_w, wkv_a_b, kvn_g, kvn_b, wk_w, wk_b, wv_w, wv_b, cos, sin):
    kv = (mxq(f64(x), 2, "e4m3") @ mxq(f64(wkv_a_w), 0, "e4m3")) + f64(wkv_a_b)
    k_rope = kv[..., : H * ROPE]
    c = kv[..., H * ROPE:]
    mu = c.mean(-1, keepdims=True)
    var = np.square(c - mu).mean(-1, keepdims=True)
    c = (c - mu) / np.sqrt(var + EPS) * f64(kvn_g) + f64(kvn_b)
    cq = mxq(c, 2, "e4m3")
    k_nope = (cq @ mxq(f64(wk_w), 0, "e4m3")) + f64(wk_b)
    v = (cq @ mxq(f64(wv_w), 0, "e4m3")) + f64(wv_b)
    k = np.concatenate([k_nope, k_rope], axis=-1).reshape(B, S, H, QKHD)
    k = np.concatenate([k[..., :NOPE], rope(k[..., NOPE:], f64(cos), f64(sin))], axis=-1)
    return k, v.reshape(B, S, H, VHD)


def e4m3fn_bytes(y):
    return np.clip(np.asarray(y, np.float64), -448.0, 448.0).astype(np.float32).astype(ml_dtypes.float8_e4m3fn).view(np.uint8)


def e4m3fn_values(b):
    return np.asarray(b, np.uint8).view(ml_dtypes.float8_e4m3fn).astype(np.float64)


def setup_inputs():
    d = draw0()
    x0 = np.asarray(d['x']).astype(np.float64)
    s = (np.max(np.abs(x0), axis=(0, 1), keepdims=True) / 448.0).astype(np.float32)
    out = {}
    for k, v in d.items():
        if k == 'x':
            out['x_bytes'] = e4m3fn_bytes(x0 / s.astype(np.float64))
            out['x_scale'] = s
        else:
            out[k] = v
    return out


def reference(x_bytes, x_scale, wkv_a_w, wkv_a_b, kvn_g, kvn_b, wk_w, wk_b, wv_w, wv_b, cos, sin):
    return core(e4m3fn_values(x_bytes) * x_scale.astype(np.float64), wkv_a_w, wkv_a_b, kvn_g, kvn_b, wk_w, wk_b, wv_w, wv_b, cos, sin)

@@ -1,0 +1,408 @@
+from contextlib import ExitStack
+
+import concourse.mybir as mybir
+from concourse.masks import make_identity
+
+B, S, DIM, H, NOPE, ROPE, VHD = 4, 2048, 512, 2, 128, 64, 128
+KV_RANK = 512
+N_ROPE = H * ROPE
+N_K = H * NOPE
+N_V = H * VHD
+QKHD = NOPE + ROPE
+EPS = 1e-5
+
+FLOPS = 2 * B * S * DIM * (N_ROPE + KV_RANK) + 2 * B * S * KV_RANK * (N_K + N_V)
+
+F32 = mybir.dt.float32
+BF16 = mybir.dt.bfloat16
+U32 = mybir.dt.uint32
+U8 = mybir.dt.uint8
+FP8 = mybir.dt.float8_e4m3fn
+FP8X4 = mybir.dt.float8_e4m3fn_x4
+ALU = mybir.AluOpType
+ACT = mybir.ActivationFunctionType
+
+P = 128
+J = S // P
+PAIR = 2
+N_PAIRS = B * J // PAIR
+W = PAIR * P
+
+
+def tile_mla_pa_t_kernel(
+    tc, x_bytes, x_scale, wkv_a_w, wkv_a_b, kvn_g, kvn_b, wk_w, wk_b, wv_w, wv_b, cos, sin, out_0, out_1
+):
+    nc = tc.nc
+    x_view = x_bytes.rearrange("b (p j) k -> b p j k", p=P)
+    k_view = out_0.rearrange("b (p j) h d -> b p j (h d)", p=P)
+    v_view = out_1.rearrange("b (p j) h d -> b p j (h d)", p=P)
+
+    with ExitStack() as ctx:
+        keep = ctx.enter_context(tc.tile_pool(name="keep", bufs=1))
+        two = ctx.enter_context(tc.tile_pool(name="two", bufs=2))
+        three = ctx.enter_context(tc.tile_pool(name="three", bufs=3))
+        stages = ctx.enter_context(tc.tile_pool(name="stages", bufs=6))
+        small = ctx.enter_context(tc.tile_pool(name="small", bufs=4))
+        ps_x = ctx.enter_context(tc.psum_pool(name="ps_x", bufs=2))
+        ps_mm = ctx.enter_context(tc.psum_pool(name="ps_mm", bufs=4))
+        ps_z = ctx.enter_context(tc.psum_pool(name="ps_z", bufs=2))
+        ctx.enter_context(tc.manual_schedule())
+
+        groups = [1, 1, 2, 4] + [4, 4] * 3
+        where = {}
+        byte_tiles = []
+        m = 0
+        for gi, n in enumerate(groups):
+            t = keep.tile([P, n * PAIR * DIM], U8, name="xbytes%d" % gi, align_bytes=64)
+            for q in range(n):
+                where[m + q] = (gi, q)
+            byte_tiles.append((t, m, n))
+            m += n
+
+        def load_group(gi):
+            t, m0, n = byte_tiles[gi]
+            b, j0 = m0 // (J // PAIR), PAIR * (m0 % (J // PAIR))
+            nc.sync.dma_start(
+                out=t[:].rearrange("p (j k) -> p j k", k=DIM), in_=x_view[b][:, j0 : j0 + n * PAIR, :]
+            )
+
+        wa_raw = keep.tile([P, 4, N_ROPE + KV_RANK], BF16)
+        sc = keep.tile([P, 4], F32)
+        wk_raw = keep.tile([P, 4, N_K], BF16)
+        wv_raw = keep.tile([P, 4, N_V], BF16)
+        cos_raw = keep.tile([P, J * ROPE // 2], BF16)
+        sin_raw = keep.tile([P, J * ROPE // 2], BF16)
+        bias_a = keep.tile([P, N_ROPE + KV_RANK], BF16)
+        bias_o = keep.tile([P, N_K + N_V], BF16)
+        g_raw = keep.tile([P, 4], BF16)
+        b_raw = keep.tile([P, 4], BF16)
+
+        load_group(0)
+        nc.sync.dma_start(out=wa_raw[:], in_=wkv_a_w.rearrange("(p j) n -> p j n", j=4))
+        load_group(1)
+        nc.sync.dma_start(out=cos_raw[:], in_=cos.rearrange("(p j) a -> p (j a)", p=P))
+        nc.sync.dma_start(out=sin_raw[:], in_=sin.rearrange("(p j) a -> p (j a)", p=P))
+        nc.sync.dma_start(out=wk_raw[:], in_=wk_w.rearrange("(p j) n -> p j n", j=4))
+        nc.sync.dma_start(out=wv_raw[:], in_=wv_w.rearrange("(p j) n -> p j n", j=4))
+        for gi in range(2, len(groups)):
+            load_group(gi)
+        nc.scalar.dma_start(out=sc[:], in_=x_scale.rearrange("a b (p t) -> p (a b t)", t=4))
+        nc.scalar.dma_start(out=bias_a[:], in_=wkv_a_b.partition_broadcast(P))
+        nc.scalar.dma_start(out=g_raw[:], in_=kvn_g.rearrange("(p t) -> p t", t=4))
+        nc.scalar.dma_start(out=b_raw[:], in_=kvn_b.rearrange("(p t) -> p t", t=4))
+        nc.scalar.dma_start(out=bias_o[:, 0:N_K], in_=wk_b.partition_broadcast(P))
+        nc.scalar.dma_start(out=bias_o[:, N_K:], in_=wv_b.partition_broadcast(P))
+
+        warm = keep.tile([P, 1], F32)
+        warm_out = keep.tile([P, 1], F32)
+        nc.vector.memset(warm[:], 0.0)
+        nc.scalar.activation(warm_out[:], warm[:], ACT.Square)
+        ident = keep.tile([P, P], F32)
+        make_identity(nc, ident[:])
+        minus_half = keep.tile([P, PAIR], F32)
+        nc.gpsimd.memset(minus_half[:], -0.5)
+        rot_c = keep.tile([P, J, ROPE], F32)
+        rot_s = keep.tile([P, J, ROPE], F32)
+        c_pairs = rot_c[:].rearrange("p j (a e) -> p (j a) e", e=2)
+        s_pairs = rot_s[:].rearrange("p j (a e) -> p (j a) e", e=2)
+        nc.gpsimd.tensor_scalar(c_pairs[:, :, 0], cos_raw[:], 1.0, 0.0, ALU.mult, ALU.add)
+        nc.gpsimd.tensor_scalar(c_pairs[:, :, 1], cos_raw[:], 1.0, 0.0, ALU.mult, ALU.add)
+        nc.gpsimd.tensor_scalar(s_pairs[:, :, 0], sin_raw[:], -1.0, 0.0, ALU.mult, ALU.add)
+        nc.gpsimd.tensor_scalar(s_pairs[:, :, 1], sin_raw[:], 1.0, 0.0, ALU.mult, ALU.add)
+
+        wa_g = keep.tile([P, N_ROPE + KV_RANK, 4], BF16, align_bytes=64)
+        wa_q = keep.tile([P, KV_RANK + N_ROPE], U32, align_bytes=64)
+        wa_s = keep.tile([P, KV_RANK + N_ROPE], U8, align_bytes=64)
+        w2_g = keep.tile([P, N_K + N_V, 4], BF16, align_bytes=64)
+        w2_q = keep.tile([P, N_K + N_V], U32, align_bytes=64)
+        w2_s = keep.tile([P, N_K + N_V], U8, align_bytes=64)
+        ba = keep.tile([P, KV_RANK], F32)
+        g4 = keep.tile([P, 4], F32)
+        b4 = keep.tile([P, 4], F32)
+
+        def quantize(codes, scales, grouped):
+            nc.vector.quantize_mx(
+                out=codes.bitcast(FP8X4), scales=scales, in_=grouped.rearrange("p n j -> p (n j)")
+            )
+
+        def prep_first_weights():
+            nc.vector.tensor_copy(
+                out=wa_g[:, 0:KV_RANK, :].rearrange("p (t m) j -> p t m j", t=4),
+                in_=wa_raw[:, :, N_ROPE:].rearrange("p j (m t) -> p t m j", t=4),
+            )
+            nc.scalar.copy(
+                out=wa_g[:, KV_RANK:, :], in_=wa_raw[:, :, 0:N_ROPE].rearrange("p j n -> p n j")
+            )
+            quantize(wa_q[:, 0:KV_RANK], wa_s[:, 0:KV_RANK], wa_g[:, 0:KV_RANK, :])
+            quantize(wa_q[:, KV_RANK:], wa_s[:, KV_RANK:], wa_g[:, KV_RANK:, :])
+
+        def prep_small():
+            nc.scalar.copy(
+                out=ba[:].rearrange("p (t m) -> p t m", t=4),
+                in_=bias_a[:, N_ROPE:].rearrange("p (m t) -> p t m", t=4),
+            )
+            nc.scalar.copy(out=g4[:], in_=g_raw[:])
+            nc.scalar.copy(out=b4[:], in_=b_raw[:])
+
+        def prep_second_weights():
+            nc.scalar.copy(out=w2_g[:, 0:N_K, :], in_=wk_raw[:].rearrange("p j n -> p n j"))
+            nc.scalar.copy(out=w2_g[:, N_K:, :], in_=wv_raw[:].rearrange("p j n -> p n j"))
+
+        st = {}
+
+        def get(m, key):
+            return st[(m, key)]
+
+        def widen(m):
+            gi, q = where[m]
+            xb = three.tile([P, PAIR * DIM], BF16, name="xb", align_bytes=64)
+            src = byte_tiles[gi][0][:, q * PAIR * DIM : (q + 1) * PAIR * DIM]
+            nc.scalar.copy(out=xb[:], in_=src.bitcast(FP8))
+            st[(m, "xb")] = xb
+
+        def turn_x(m):
+            words = get(m, "xb")[:].bitcast(F32)
+            xt = ps_x.tile([P, 2 * W], F32, name="xt")
+            for i in range(PAIR):
+                for u in range(2):
+                    nc.tensor.transpose(
+                        xt[:, u * W + i * P : u * W + (i + 1) * P],
+                        words[:, 256 * i + u : 256 * (i + 1) : 2],
+                        ident[:],
+                    )
+            st[(m, "xt")] = xt
+
+        def scale_x(m):
+            xg = two.tile([P, W, 4], BF16, name="xg", align_bytes=64)
+            nc.vector.tensor_tensor(
+                out=xg[:].rearrange("p q (u e) -> p q u e", u=2),
+                in0=get(m, "xt")[:].bitcast(BF16).rearrange("p (u q e) -> p q u e", u=2, e=2),
+                in1=sc[:].rearrange("p (o u e) -> p o u e", o=1, u=2).to_broadcast([P, W, 2, 2]),
+                op=ALU.mult,
+            )
+            st[(m, "xg")] = xg
+
+        def quant_x(m):
+            xq = three.tile([P, W], U32, name="xq", align_bytes=64)
+            xs = three.tile([P, W], U8, name="xs", align_bytes=64)
+            quantize(xq[:], xs[:], get(m, "xg")[:])
+            st[(m, "xq")] = (xq, xs)
+
+        def mx(out, codes, scales, i, wq, ws, c0, c1):
+            nc.tensor.matmul_mx(
+                out=out,
+                lhsT=codes[:, i * P : (i + 1) * P].bitcast(FP8X4),
+                lhsT_scale=scales[:, i * P : (i + 1) * P],
+                rhs=wq[:, c0:c1].bitcast(FP8X4),
+                rhs_scale=ws[:, c0:c1],
+                start=True,
+                stop=True,
+            )
+
+        def first_product(m):
+            xq, xs = get(m, "xq")
+            banks = []
+            for i in range(PAIR):
+                bank = ps_mm.tile([P, 512], F32, name="mm")
+                mx(bank[:], xq, xs, i, wa_q, wa_s, 0, KV_RANK)
+                banks.append(bank)
+            bank = ps_mm.tile([P, 512], F32, name="mm")
+            for i in range(PAIR):
+                mx(bank[:, i * P : (i + 1) * P], xq, xs, i, wa_q, wa_s, KV_RANK, KV_RANK + N_ROPE)
+            banks.append(bank)
+            st[(m, "first")] = banks
+            st[(m, "c")] = three.tile([P, PAIR, KV_RANK], F32, name="c")
+            st[(m, "sums")] = small.tile([P, PAIR], F32, name="sums")
+
+        def latent(m, i):
+            nc.vector.scalar_tensor_tensor(
+                out=get(m, "c")[:, i, :],
+                in0=get(m, "first")[i][:],
+                scalar=1.0,
+                in1=ba[:],
+                op0=ALU.mult,
+                op1=ALU.add,
+                accum_out=get(m, "sums")[:, i : i + 1],
+            )
+
+        def rope_bias(m):
+            stage = stages.tile([P, 1664], F32, name="stage")
+            nc.vector.tensor_tensor(
+                out=stage[:, 0 : PAIR * H * QKHD].rearrange("p (i c) -> p i c", i=PAIR)[:, :, N_K:],
+                in0=get(m, "first")[PAIR][:, 0:W].rearrange("p (i c) -> p i c", i=PAIR),
+                in1=bias_a[:, 0:N_ROPE].rearrange("p (o c) -> p o c", o=1).to_broadcast([P, PAIR, N_ROPE]),
+                op=ALU.add,
+            )
+            st[(m, "stage")] = stage
+
+        def squares(m):
+            minus_mu = small.tile([P, PAIR], F32, name="minus_mu")
+            nc.scalar.activation(minus_mu[:], get(m, "sums")[:], ACT.Copy, scale=-1.0 / KV_RANK)
+            ss = small.tile([P, PAIR], F32, name="ss")
+            for i in range(PAIR):
+                junk = two.tile([P, KV_RANK], BF16, name="junk")
+                nc.scalar.activation(
+                    junk[:],
+                    get(m, "c")[:, i, :],
+                    ACT.Square,
+                    bias=minus_mu[:, i : i + 1],
+                    accum_out=ss[:, i : i + 1],
+                )
+            st[(m, "minus_mu")] = minus_mu
+            st[(m, "ss")] = ss
+
+        def stats(m):
+            var = small.tile([P, PAIR], F32, name="var")
+            rstd = small.tile([P, PAIR], F32, name="rstd")
+            shift = small.tile([P, PAIR], F32, name="shift")
+            nc.gpsimd.tensor_scalar(var[:], get(m, "ss")[:], 1.0 / KV_RANK, EPS, ALU.mult, ALU.add)
+            nc.gpsimd.tensor_tensor(out=rstd[:], in0=var[:], in1=minus_half[:], op=ALU.pow)
+            nc.gpsimd.tensor_tensor(out=shift[:], in0=get(m, "minus_mu")[:], in1=rstd[:], op=ALU.mult)
+            st[(m, "rstd")] = rstd
+            st[(m, "shift")] = shift
+
+        def norm(m):
+            z = two.tile([P, PAIR, KV_RANK], F32, name="z")
+            for i in range(PAIR):
+                nc.gpsimd.tensor_scalar(
+                    z[:, i, :],
+                    get(m, "c")[:, i, :],
+                    get(m, "rstd")[:, i : i + 1],
+                    get(m, "shift")[:, i : i + 1],
+                    ALU.mult,
+                    ALU.add,
+                )
+            st[(m, "z")] = z
+
+        def turn_z(m):
+            z = get(m, "z")
+            banks = []
+            for h in range(2):
+                zt = ps_z.tile([P, 2, W], F32, name="zt")
+                for i in range(PAIR):
+                    for tt in range(2):
+                        t = 2 * h + tt
+                        nc.tensor.transpose(
+                            zt[:, tt, i * P : (i + 1) * P], z[:, i, t * P : (t + 1) * P], ident[:]
+                        )
+                banks.append(zt)
+            st[(m, "zt")] = banks
+
+        def gain(m):
+            planes = two.tile([P, 4, W], BF16, name="planes")
+            for t in range(4):
+                nc.scalar.activation(
+                    planes[:, t, :],
+                    get(m, "zt")[t // 2][:, t % 2, :],
+                    ACT.Identity,
+                    bias=b4[:, t : t + 1],
+                    scale=g4[:, t : t + 1],
+                )
+            st[(m, "planes")] = planes
+
+        def interleave(m):
+            zg = two.tile([P, W, 4], BF16, name="zg", align_bytes=64)
+            nc.scalar.copy(out=zg[:], in_=get(m, "planes")[:].rearrange("p t n -> p n t"))
+            st[(m, "zg")] = zg
+
+        def quant_z(m):
+            zq = three.tile([P, W], U32, name="zq", align_bytes=64)
+            zs = three.tile([P, W], U8, name="zs", align_bytes=64)
+            quantize(zq[:], zs[:], get(m, "zg")[:])
+            st[(m, "zq")] = (zq, zs)
+
+        def second_product(m):
+            zq, zs = get(m, "zq")
+            banks = []
+            for i in range(PAIR):
+                bank = ps_mm.tile([P, 512], F32, name="mm")
+                mx(bank[:], zq, zs, i, w2_q, w2_s, 0, 512)
+                banks.append(bank)
+            st[(m, "second")] = banks
+
+        def out_bias(m, i):
+            a, s = i * H * QKHD, PAIR * H * QKHD - i * P
+            nc.vector.tensor_tensor(
+                out=get(m, "stage")[:, a : a + 2 * s].rearrange("p (r x) -> p r x", r=2)[:, :, 0:256],
+                in0=get(m, "second")[i][:].rearrange("p (r x) -> p r x", r=2),
+                in1=bias_o[:].rearrange("p (r x) -> p r x", r=2),
+                op=ALU.add,
+            )
+
+        def rotate(m):
+            j0 = PAIR * (m % (J // PAIR))
+            rot = get(m, "stage")[:, 0 : PAIR * H * QKHD].rearrange("p (j h c) -> p j h c", j=PAIR, h=H)[
+                :, :, :, NOPE:
+            ]
+            shape = [P, PAIR, H, ROPE]
+            t1 = two.tile(shape, F32, name="t1")
+            t2 = two.tile(shape, F32, name="t2")
+
+            def table(tab):
+                return tab[:, j0 : j0 + PAIR, :].rearrange("p j (o c) -> p j o c", o=1).to_broadcast(shape)
+
+            nc.gpsimd.tensor_tensor(out=t1[:], in0=rot, in1=table(rot_c), op=ALU.mult)
+            nc.gpsimd.tensor_tensor(
+                out=t2[:].rearrange("p j h (a e) -> p j h a e", e=2),
+                in0=rot.rearrange("p j h (a e) -> p j h a e", e=2)[:, :, :, :, ::-1],
+                in1=table(rot_s).rearrange("p j h (a e) -> p j h a e", e=2),
+                op=ALU.mult,
+            )
+            nc.gpsimd.tensor_tensor(out=rot, in0=t1[:], in1=t2[:], op=ALU.add)
+
+        def store(m):
+            b, j0 = m // (J // PAIR), PAIR * (m % (J // PAIR))
+            stage = get(m, "stage")
+            n_k = PAIR * H * QKHD
+            nc.sync.dma_start(
+                out=k_view[b][:, j0 : j0 + PAIR, :], in_=stage[:, 0:n_k].rearrange("p (j c) -> p j c", j=PAIR)
+            )
+            nc.sync.dma_start(
+                out=v_view[b][:, j0 : j0 + PAIR, :],
+                in_=stage[:, n_k : n_k + PAIR * N_V].rearrange("p (j c) -> p j c", j=PAIR),
+            )
+
+        def live(m):
+            return 0 <= m < N_PAIRS
+
+        for it in range(N_PAIRS + 7):
+            if live(it - 3):
+                stats(it - 3)
+                norm(it - 3)
+            if live(it - 6):
+                rotate(it - 6)
+                store(it - 6)
+            if live(it - 5):
+                second_product(it - 5)
+            if live(it - 2):
+                first_product(it - 2)
+            for i in range(PAIR):
+                if live(it - 5):
+                    out_bias(it - 5, i)
+                if live(it - 2):
+                    latent(it - 2, i)
+            if live(it - 2):
+                rope_bias(it - 2)
+            if live(it):
+                widen(it)
+            if it == 0:
+                prep_first_weights()
+            if it == 1:
+                prep_small()
+                prep_second_weights()
+            if live(it - 4):
+                interleave(it - 4)
+            if live(it - 2):
+                squares(it - 2)
+            if live(it - 1):
+                turn_x(it - 1)
+                scale_x(it - 1)
+            if live(it - 3):
+                turn_z(it - 3)
+                gain(it - 3)
+            if it == 2:
+                quantize(w2_q[:], w2_s[:], w2_g[:])
+            if live(it - 4):
+                quant_z(it - 4)
+            if live(it - 1):
+                quant_x(it - 1)

@@ -26,6 +26,7 @@ P = 128
 J = S // P
 PAIR = 2
 N_PAIRS = B * J // PAIR
+REPEAT_1, REPEAT_2 = 0, 0
 W = PAIR * P
 
 
@@ -77,21 +78,23 @@ def tile_mla_pa_t_kernel(
         g_raw = keep.tile([P, 4], BF16)
         b_raw = keep.tile([P, 4], BF16)
 
+        nc.sync.dma_start(out=sc[:], in_=x_scale.rearrange("a b (p t) -> p (a b t)", t=4))
         load_group(0)
         nc.sync.dma_start(out=wa_raw[:], in_=wkv_a_w.rearrange("(p j) n -> p j n", j=4))
+        nc.scalar.dma_start(out=bias_a[:], in_=wkv_a_b.partition_broadcast(P))
         load_group(1)
-        nc.sync.dma_start(out=cos_raw[:], in_=cos.rearrange("(p j) a -> p (j a)", p=P))
-        nc.sync.dma_start(out=sin_raw[:], in_=sin.rearrange("(p j) a -> p (j a)", p=P))
+        load_group(2)
         nc.sync.dma_start(out=wk_raw[:], in_=wk_w.rearrange("(p j) n -> p j n", j=4))
         nc.sync.dma_start(out=wv_raw[:], in_=wv_w.rearrange("(p j) n -> p j n", j=4))
-        for gi in range(2, len(groups)):
-            load_group(gi)
-        nc.scalar.dma_start(out=sc[:], in_=x_scale.rearrange("a b (p t) -> p (a b t)", t=4))
-        nc.scalar.dma_start(out=bias_a[:], in_=wkv_a_b.partition_broadcast(P))
         nc.scalar.dma_start(out=g_raw[:], in_=kvn_g.rearrange("(p t) -> p t", t=4))
         nc.scalar.dma_start(out=b_raw[:], in_=kvn_b.rearrange("(p t) -> p t", t=4))
+        nc.sync.dma_start(out=cos_raw[:], in_=cos.rearrange("(p j) a -> p (j a)", p=P))
+        nc.sync.dma_start(out=sin_raw[:], in_=sin.rearrange("(p j) a -> p (j a)", p=P))
+        load_group(3)
         nc.scalar.dma_start(out=bias_o[:, 0:N_K], in_=wk_b.partition_broadcast(P))
         nc.scalar.dma_start(out=bias_o[:, N_K:], in_=wv_b.partition_broadcast(P))
+        for gi in range(4, len(groups)):
+            load_group(gi)
 
         warm = keep.tile([P, 1], F32)
         warm_out = keep.tile([P, 1], F32)
@@ -99,8 +102,6 @@ def tile_mla_pa_t_kernel(
         nc.scalar.activation(warm_out[:], warm[:], ACT.Square)
         ident = keep.tile([P, P], F32)
         make_identity(nc, ident[:])
-        minus_half = keep.tile([P, PAIR], F32)
-        nc.gpsimd.memset(minus_half[:], -0.5)
         rot_c = keep.tile([P, J, ROPE], F32)
         rot_s = keep.tile([P, J, ROPE], F32)
         c_pairs = rot_c[:].rearrange("p j (a e) -> p (j a) e", e=2)
@@ -204,7 +205,8 @@ def tile_mla_pa_t_kernel(
             banks = []
             for i in range(PAIR):
                 bank = ps_mm.tile([P, 512], F32, name="mm")
-                mx(bank[:], xq, xs, i, wa_q, wa_s, 0, KV_RANK)
+                for again in range(1 + (i < REPEAT_1)):
+                    mx(bank[:], xq, xs, i, wa_q, wa_s, 0, KV_RANK)
                 banks.append(bank)
             bank = ps_mm.tile([P, 512], F32, name="mm")
             for i in range(PAIR):
@@ -236,8 +238,6 @@ def tile_mla_pa_t_kernel(
             st[(m, "stage")] = stage
 
         def squares(m):
-            minus_mu = small.tile([P, PAIR], F32, name="minus_mu")
-            nc.scalar.activation(minus_mu[:], get(m, "sums")[:], ACT.Copy, scale=-1.0 / KV_RANK)
             ss = small.tile([P, PAIR], F32, name="ss")
             for i in range(PAIR):
                 junk = two.tile([P, KV_RANK], BF16, name="junk")
@@ -245,32 +245,30 @@ def tile_mla_pa_t_kernel(
                     junk[:],
                     get(m, "c")[:, i, :],
                     ACT.Square,
-                    bias=minus_mu[:, i : i + 1],
+                    bias=get(m, "sums")[:, i : i + 1],
+                    scale=-float(KV_RANK),
                     accum_out=ss[:, i : i + 1],
                 )
-            st[(m, "minus_mu")] = minus_mu
             st[(m, "ss")] = ss
 
         def stats(m):
-            var = small.tile([P, PAIR], F32, name="var")
+            mean = small.tile([P, PAIR], F32, name="mean")
             rstd = small.tile([P, PAIR], F32, name="rstd")
-            shift = small.tile([P, PAIR], F32, name="shift")
-            nc.gpsimd.tensor_scalar(var[:], get(m, "ss")[:], 1.0 / KV_RANK, EPS, ALU.mult, ALU.add)
-            nc.gpsimd.tensor_tensor(out=rstd[:], in0=var[:], in1=minus_half[:], op=ALU.pow)
-            nc.gpsimd.tensor_tensor(out=shift[:], in0=get(m, "minus_mu")[:], in1=rstd[:], op=ALU.mult)
+            nc.scalar.activation(mean[:], get(m, "sums")[:], ACT.Copy, scale=1.0 / KV_RANK)
+            nc.scalar.activation(rstd[:], get(m, "ss")[:], ACT.Abs_reciprocal_sqrt, bias=EPS, scale=1.0 / KV_RANK**3)
             st[(m, "rstd")] = rstd
-            st[(m, "shift")] = shift
+            st[(m, "mean")] = mean
 
         def norm(m):
             z = two.tile([P, PAIR, KV_RANK], F32, name="z")
             for i in range(PAIR):
-                nc.gpsimd.tensor_scalar(
+                nc.vector.tensor_scalar(
                     z[:, i, :],
                     get(m, "c")[:, i, :],
+                    get(m, "mean")[:, i : i + 1],
                     get(m, "rstd")[:, i : i + 1],
-                    get(m, "shift")[:, i : i + 1],
+                    ALU.subtract,
                     ALU.mult,
-                    ALU.add,
                 )
             st[(m, "z")] = z
 
@@ -302,7 +300,10 @@ def tile_mla_pa_t_kernel(
 
         def interleave(m):
             zg = two.tile([P, W, 4], BF16, name="zg", align_bytes=64)
-            nc.scalar.copy(out=zg[:], in_=get(m, "planes")[:].rearrange("p t n -> p n t"))
+            nc.scalar.copy(
+                out=zg[:].rearrange("p (c i) t -> p c t i", i=4),
+                in_=get(m, "planes")[:].rearrange("p t (c i) -> p c t i", i=4),
+            )
             st[(m, "zg")] = zg
 
         def quant_z(m):
@@ -316,7 +317,8 @@ def tile_mla_pa_t_kernel(
             banks = []
             for i in range(PAIR):
                 bank = ps_mm.tile([P, 512], F32, name="mm")
-                mx(bank[:], zq, zs, i, w2_q, w2_s, 0, 512)
+                for again in range(1 + (i < REPEAT_2)):
+                    mx(bank[:], zq, zs, i, w2_q, w2_s, 0, 512)
                 banks.append(bank)
             st[(m, "second")] = banks
 
@@ -365,24 +367,29 @@ def tile_mla_pa_t_kernel(
         def live(m):
             return 0 <= m < N_PAIRS
 
-        for it in range(N_PAIRS + 7):
-            if live(it - 3):
-                stats(it - 3)
-                norm(it - 3)
-            if live(it - 6):
-                rotate(it - 6)
-                store(it - 6)
+        for it in range(N_PAIRS + 6):
+            if it >= N_PAIRS and live(it - 4):
+                norm(it - 4)
+            if live(it - 5):
+                quant_z(it - 5)
+            if live(it - 2):
+                quant_x(it - 2)
+            if it == 2:
+                quantize(w2_q[:], w2_s[:], w2_g[:])
+            if live(it - 1):
+                turn_x(it - 1)
             if live(it - 5):
                 second_product(it - 5)
-            if live(it - 2):
-                first_product(it - 2)
-            for i in range(PAIR):
-                if live(it - 5):
+            if live(it - 3):
+                squares(it - 3)
+                stats(it - 3)
+            if it < N_PAIRS and live(it - 4):
+                norm(it - 4)
+            if live(it - 5):
+                for i in range(PAIR):
                     out_bias(it - 5, i)
-                if live(it - 2):
-                    latent(it - 2, i)
-            if live(it - 2):
-                rope_bias(it - 2)
+                rotate(it - 5)
+                store(it - 5)
             if live(it):
                 widen(it)
             if it == 0:
@@ -391,18 +398,15 @@ def tile_mla_pa_t_kernel(
                 prep_small()
                 prep_second_weights()
             if live(it - 4):
-                interleave(it - 4)
-            if live(it - 2):
-                squares(it - 2)
+                turn_z(it - 4)
             if live(it - 1):
-                turn_x(it - 1)
                 scale_x(it - 1)
-            if live(it - 3):
-                turn_z(it - 3)
-                gain(it - 3)
-            if it == 2:
-                quantize(w2_q[:], w2_s[:], w2_g[:])
             if live(it - 4):
-                quant_z(it - 4)
-            if live(it - 1):
-                quant_x(it - 1)
+                gain(it - 4)
+            if live(it - 2):
+                first_product(it - 2)
+                for i in range(PAIR):
+                    latent(it - 2, i)
+                rope_bias(it - 2)
+            if live(it - 4):
+                interleave(it - 4)

from contextlib import ExitStack

import concourse.mybir as mybir
from concourse.masks import make_identity

B, S, DIM, H, NOPE, ROPE, VHD = 4, 2048, 512, 2, 128, 64, 128
KV_RANK = 512
N_ROPE = H * ROPE
N_K = H * NOPE
N_V = H * VHD
QKHD = NOPE + ROPE
EPS = 1e-5

FLOPS = 2 * B * S * DIM * (N_ROPE + KV_RANK) + 2 * B * S * KV_RANK * (N_K + N_V)

F32 = mybir.dt.float32
BF16 = mybir.dt.bfloat16
U32 = mybir.dt.uint32
U8 = mybir.dt.uint8
FP8 = mybir.dt.float8_e4m3fn
FP8X4 = mybir.dt.float8_e4m3fn_x4
ALU = mybir.AluOpType
ACT = mybir.ActivationFunctionType

P = 128
J = S // P
PAIR = 2
N_PAIRS = B * J // PAIR
REPEAT_1, REPEAT_2 = 0, 0
W = PAIR * P


def tile_mla_pa_t_kernel(
    tc, x_bytes, x_scale, wkv_a_w, wkv_a_b, kvn_g, kvn_b, wk_w, wk_b, wv_w, wv_b, cos, sin, out_0, out_1
):
    nc = tc.nc
    x_view = x_bytes.rearrange("b (p j) k -> b p j k", p=P)
    k_view = out_0.rearrange("b (p j) h d -> b p j (h d)", p=P)
    v_view = out_1.rearrange("b (p j) h d -> b p j (h d)", p=P)

    with ExitStack() as ctx:
        keep = ctx.enter_context(tc.tile_pool(name="keep", bufs=1))
        two = ctx.enter_context(tc.tile_pool(name="two", bufs=2))
        three = ctx.enter_context(tc.tile_pool(name="three", bufs=3))
        stages = ctx.enter_context(tc.tile_pool(name="stages", bufs=6))
        small = ctx.enter_context(tc.tile_pool(name="small", bufs=4))
        ps_x = ctx.enter_context(tc.psum_pool(name="ps_x", bufs=2))
        ps_mm = ctx.enter_context(tc.psum_pool(name="ps_mm", bufs=4))
        ps_z = ctx.enter_context(tc.psum_pool(name="ps_z", bufs=2))
        ctx.enter_context(tc.manual_schedule())

        groups = [1, 1, 2, 4] + [4, 4] * 3
        where = {}
        byte_tiles = []
        m = 0
        for gi, n in enumerate(groups):
            t = keep.tile([P, n * PAIR * DIM], U8, name="xbytes%d" % gi, align_bytes=64)
            for q in range(n):
                where[m + q] = (gi, q)
            byte_tiles.append((t, m, n))
            m += n

        def load_group(gi):
            t, m0, n = byte_tiles[gi]
            b, j0 = m0 // (J // PAIR), PAIR * (m0 % (J // PAIR))
            nc.sync.dma_start(
                out=t[:].rearrange("p (j k) -> p j k", k=DIM), in_=x_view[b][:, j0 : j0 + n * PAIR, :]
            )

        wa_raw = keep.tile([P, 4, N_ROPE + KV_RANK], BF16)
        sc = keep.tile([P, 4], F32)
        wk_raw = keep.tile([P, 4, N_K], BF16)
        wv_raw = keep.tile([P, 4, N_V], BF16)
        cos_raw = keep.tile([P, J * ROPE // 2], BF16)
        sin_raw = keep.tile([P, J * ROPE // 2], BF16)
        bias_a = keep.tile([P, N_ROPE + KV_RANK], BF16)
        bias_o = keep.tile([P, N_K + N_V], BF16)
        g_raw = keep.tile([P, 4], BF16)
        b_raw = keep.tile([P, 4], BF16)

        nc.sync.dma_start(out=sc[:], in_=x_scale.rearrange("a b (p t) -> p (a b t)", t=4))
        load_group(0)
        nc.sync.dma_start(out=wa_raw[:], in_=wkv_a_w.rearrange("(p j) n -> p j n", j=4))
        nc.scalar.dma_start(out=bias_a[:], in_=wkv_a_b.partition_broadcast(P))
        load_group(1)
        load_group(2)
        nc.sync.dma_start(out=wk_raw[:], in_=wk_w.rearrange("(p j) n -> p j n", j=4))
        nc.sync.dma_start(out=wv_raw[:], in_=wv_w.rearrange("(p j) n -> p j n", j=4))
        nc.scalar.dma_start(out=g_raw[:], in_=kvn_g.rearrange("(p t) -> p t", t=4))
        nc.scalar.dma_start(out=b_raw[:], in_=kvn_b.rearrange("(p t) -> p t", t=4))
        nc.sync.dma_start(out=cos_raw[:], in_=cos.rearrange("(p j) a -> p (j a)", p=P))
        nc.sync.dma_start(out=sin_raw[:], in_=sin.rearrange("(p j) a -> p (j a)", p=P))
        load_group(3)
        nc.scalar.dma_start(out=bias_o[:, 0:N_K], in_=wk_b.partition_broadcast(P))
        nc.scalar.dma_start(out=bias_o[:, N_K:], in_=wv_b.partition_broadcast(P))
        for gi in range(4, len(groups)):
            load_group(gi)

        warm = keep.tile([P, 1], F32)
        warm_out = keep.tile([P, 1], F32)
        nc.vector.memset(warm[:], 0.0)
        nc.scalar.activation(warm_out[:], warm[:], ACT.Square)
        ident = keep.tile([P, P], F32)
        make_identity(nc, ident[:])
        rot_c = keep.tile([P, J, ROPE], F32)
        rot_s = keep.tile([P, J, ROPE], F32)
        c_pairs = rot_c[:].rearrange("p j (a e) -> p (j a) e", e=2)
        s_pairs = rot_s[:].rearrange("p j (a e) -> p (j a) e", e=2)
        nc.gpsimd.tensor_scalar(c_pairs[:, :, 0], cos_raw[:], 1.0, 0.0, ALU.mult, ALU.add)
        nc.gpsimd.tensor_scalar(c_pairs[:, :, 1], cos_raw[:], 1.0, 0.0, ALU.mult, ALU.add)
        nc.gpsimd.tensor_scalar(s_pairs[:, :, 0], sin_raw[:], -1.0, 0.0, ALU.mult, ALU.add)
        nc.gpsimd.tensor_scalar(s_pairs[:, :, 1], sin_raw[:], 1.0, 0.0, ALU.mult, ALU.add)

        wa_g = keep.tile([P, N_ROPE + KV_RANK, 4], BF16, align_bytes=64)
        wa_q = keep.tile([P, KV_RANK + N_ROPE], U32, align_bytes=64)
        wa_s = keep.tile([P, KV_RANK + N_ROPE], U8, align_bytes=64)
        w2_g = keep.tile([P, N_K + N_V, 4], BF16, align_bytes=64)
        w2_q = keep.tile([P, N_K + N_V], U32, align_bytes=64)
        w2_s = keep.tile([P, N_K + N_V], U8, align_bytes=64)
        ba = keep.tile([P, KV_RANK], F32)
        g4 = keep.tile([P, 4], F32)
        b4 = keep.tile([P, 4], F32)

        def quantize(codes, scales, grouped):
            nc.vector.quantize_mx(
                out=codes.bitcast(FP8X4), scales=scales, in_=grouped.rearrange("p n j -> p (n j)")
            )

        def prep_first_weights():
            nc.vector.tensor_copy(
                out=wa_g[:, 0:KV_RANK, :].rearrange("p (t m) j -> p t m j", t=4),
                in_=wa_raw[:, :, N_ROPE:].rearrange("p j (m t) -> p t m j", t=4),
            )
            nc.scalar.copy(
                out=wa_g[:, KV_RANK:, :], in_=wa_raw[:, :, 0:N_ROPE].rearrange("p j n -> p n j")
            )
            quantize(wa_q[:, 0:KV_RANK], wa_s[:, 0:KV_RANK], wa_g[:, 0:KV_RANK, :])
            quantize(wa_q[:, KV_RANK:], wa_s[:, KV_RANK:], wa_g[:, KV_RANK:, :])

        def prep_small():
            nc.scalar.copy(
                out=ba[:].rearrange("p (t m) -> p t m", t=4),
                in_=bias_a[:, N_ROPE:].rearrange("p (m t) -> p t m", t=4),
            )
            nc.scalar.copy(out=g4[:], in_=g_raw[:])
            nc.scalar.copy(out=b4[:], in_=b_raw[:])

        def prep_second_weights():
            nc.scalar.copy(out=w2_g[:, 0:N_K, :], in_=wk_raw[:].rearrange("p j n -> p n j"))
            nc.scalar.copy(out=w2_g[:, N_K:, :], in_=wv_raw[:].rearrange("p j n -> p n j"))

        st = {}

        def get(m, key):
            return st[(m, key)]

        def widen(m):
            gi, q = where[m]
            xb = three.tile([P, PAIR * DIM], BF16, name="xb", align_bytes=64)
            src = byte_tiles[gi][0][:, q * PAIR * DIM : (q + 1) * PAIR * DIM]
            nc.scalar.copy(out=xb[:], in_=src.bitcast(FP8))
            st[(m, "xb")] = xb

        def turn_x(m):
            words = get(m, "xb")[:].bitcast(F32)
            xt = ps_x.tile([P, 2 * W], F32, name="xt")
            for i in range(PAIR):
                for u in range(2):
                    nc.tensor.transpose(
                        xt[:, u * W + i * P : u * W + (i + 1) * P],
                        words[:, 256 * i + u : 256 * (i + 1) : 2],
                        ident[:],
                    )
            st[(m, "xt")] = xt

        def scale_x(m):
            xg = two.tile([P, W, 4], BF16, name="xg", align_bytes=64)
            nc.vector.tensor_tensor(
                out=xg[:].rearrange("p q (u e) -> p q u e", u=2),
                in0=get(m, "xt")[:].bitcast(BF16).rearrange("p (u q e) -> p q u e", u=2, e=2),
                in1=sc[:].rearrange("p (o u e) -> p o u e", o=1, u=2).to_broadcast([P, W, 2, 2]),
                op=ALU.mult,
            )
            st[(m, "xg")] = xg

        def quant_x(m):
            xq = three.tile([P, W], U32, name="xq", align_bytes=64)
            xs = three.tile([P, W], U8, name="xs", align_bytes=64)
            quantize(xq[:], xs[:], get(m, "xg")[:])
            st[(m, "xq")] = (xq, xs)

        def mx(out, codes, scales, i, wq, ws, c0, c1):
            nc.tensor.matmul_mx(
                out=out,
                lhsT=codes[:, i * P : (i + 1) * P].bitcast(FP8X4),
                lhsT_scale=scales[:, i * P : (i + 1) * P],
                rhs=wq[:, c0:c1].bitcast(FP8X4),
                rhs_scale=ws[:, c0:c1],
                start=True,
                stop=True,
            )

        def first_product(m):
            xq, xs = get(m, "xq")
            banks = []
            for i in range(PAIR):
                bank = ps_mm.tile([P, 512], F32, name="mm")
                for again in range(1 + (i < REPEAT_1)):
                    mx(bank[:], xq, xs, i, wa_q, wa_s, 0, KV_RANK)
                banks.append(bank)
            bank = ps_mm.tile([P, 512], F32, name="mm")
            for i in range(PAIR):
                mx(bank[:, i * P : (i + 1) * P], xq, xs, i, wa_q, wa_s, KV_RANK, KV_RANK + N_ROPE)
            banks.append(bank)
            st[(m, "first")] = banks
            st[(m, "c")] = three.tile([P, PAIR, KV_RANK], F32, name="c")
            st[(m, "sums")] = small.tile([P, PAIR], F32, name="sums")

        def latent(m, i):
            nc.vector.scalar_tensor_tensor(
                out=get(m, "c")[:, i, :],
                in0=get(m, "first")[i][:],
                scalar=1.0,
                in1=ba[:],
                op0=ALU.mult,
                op1=ALU.add,
                accum_out=get(m, "sums")[:, i : i + 1],
            )

        def rope_bias(m):
            stage = stages.tile([P, 1664], F32, name="stage")
            nc.vector.tensor_tensor(
                out=stage[:, 0 : PAIR * H * QKHD].rearrange("p (i c) -> p i c", i=PAIR)[:, :, N_K:],
                in0=get(m, "first")[PAIR][:, 0:W].rearrange("p (i c) -> p i c", i=PAIR),
                in1=bias_a[:, 0:N_ROPE].rearrange("p (o c) -> p o c", o=1).to_broadcast([P, PAIR, N_ROPE]),
                op=ALU.add,
            )
            st[(m, "stage")] = stage

        def squares(m):
            ss = small.tile([P, PAIR], F32, name="ss")
            for i in range(PAIR):
                junk = two.tile([P, KV_RANK], BF16, name="junk")
                nc.scalar.activation(
                    junk[:],
                    get(m, "c")[:, i, :],
                    ACT.Square,
                    bias=get(m, "sums")[:, i : i + 1],
                    scale=-float(KV_RANK),
                    accum_out=ss[:, i : i + 1],
                )
            st[(m, "ss")] = ss

        def stats(m):
            mean = small.tile([P, PAIR], F32, name="mean")
            rstd = small.tile([P, PAIR], F32, name="rstd")
            nc.scalar.activation(mean[:], get(m, "sums")[:], ACT.Copy, scale=1.0 / KV_RANK)
            nc.scalar.activation(rstd[:], get(m, "ss")[:], ACT.Abs_reciprocal_sqrt, bias=EPS, scale=1.0 / KV_RANK**3)
            st[(m, "rstd")] = rstd
            st[(m, "mean")] = mean

        def norm(m):
            z = two.tile([P, PAIR, KV_RANK], F32, name="z")
            for i in range(PAIR):
                nc.vector.tensor_scalar(
                    z[:, i, :],
                    get(m, "c")[:, i, :],
                    get(m, "mean")[:, i : i + 1],
                    get(m, "rstd")[:, i : i + 1],
                    ALU.subtract,
                    ALU.mult,
                )
            st[(m, "z")] = z

        def turn_z(m):
            z = get(m, "z")
            banks = []
            for h in range(2):
                zt = ps_z.tile([P, 2, W], F32, name="zt")
                for i in range(PAIR):
                    for tt in range(2):
                        t = 2 * h + tt
                        nc.tensor.transpose(
                            zt[:, tt, i * P : (i + 1) * P], z[:, i, t * P : (t + 1) * P], ident[:]
                        )
                banks.append(zt)
            st[(m, "zt")] = banks

        def gain(m):
            planes = two.tile([P, 4, W], BF16, name="planes")
            for t in range(4):
                nc.scalar.activation(
                    planes[:, t, :],
                    get(m, "zt")[t // 2][:, t % 2, :],
                    ACT.Identity,
                    bias=b4[:, t : t + 1],
                    scale=g4[:, t : t + 1],
                )
            st[(m, "planes")] = planes

        def interleave(m):
            zg = two.tile([P, W, 4], BF16, name="zg", align_bytes=64)
            nc.scalar.copy(
                out=zg[:].rearrange("p (c i) t -> p c t i", i=4),
                in_=get(m, "planes")[:].rearrange("p t (c i) -> p c t i", i=4),
            )
            st[(m, "zg")] = zg

        def quant_z(m):
            zq = three.tile([P, W], U32, name="zq", align_bytes=64)
            zs = three.tile([P, W], U8, name="zs", align_bytes=64)
            quantize(zq[:], zs[:], get(m, "zg")[:])
            st[(m, "zq")] = (zq, zs)

        def second_product(m):
            zq, zs = get(m, "zq")
            banks = []
            for i in range(PAIR):
                bank = ps_mm.tile([P, 512], F32, name="mm")
                for again in range(1 + (i < REPEAT_2)):
                    mx(bank[:], zq, zs, i, w2_q, w2_s, 0, 512)
                banks.append(bank)
            st[(m, "second")] = banks

        def out_bias(m, i):
            a, s = i * H * QKHD, PAIR * H * QKHD - i * P
            nc.vector.tensor_tensor(
                out=get(m, "stage")[:, a : a + 2 * s].rearrange("p (r x) -> p r x", r=2)[:, :, 0:256],
                in0=get(m, "second")[i][:].rearrange("p (r x) -> p r x", r=2),
                in1=bias_o[:].rearrange("p (r x) -> p r x", r=2),
                op=ALU.add,
            )

        def rotate(m):
            j0 = PAIR * (m % (J // PAIR))
            rot = get(m, "stage")[:, 0 : PAIR * H * QKHD].rearrange("p (j h c) -> p j h c", j=PAIR, h=H)[
                :, :, :, NOPE:
            ]
            shape = [P, PAIR, H, ROPE]
            t1 = two.tile(shape, F32, name="t1")
            t2 = two.tile(shape, F32, name="t2")

            def table(tab):
                return tab[:, j0 : j0 + PAIR, :].rearrange("p j (o c) -> p j o c", o=1).to_broadcast(shape)

            nc.gpsimd.tensor_tensor(out=t1[:], in0=rot, in1=table(rot_c), op=ALU.mult)
            nc.gpsimd.tensor_tensor(
                out=t2[:].rearrange("p j h (a e) -> p j h a e", e=2),
                in0=rot.rearrange("p j h (a e) -> p j h a e", e=2)[:, :, :, :, ::-1],
                in1=table(rot_s).rearrange("p j h (a e) -> p j h a e", e=2),
                op=ALU.mult,
            )
            nc.gpsimd.tensor_tensor(out=rot, in0=t1[:], in1=t2[:], op=ALU.add)

        def store(m):
            b, j0 = m // (J // PAIR), PAIR * (m % (J // PAIR))
            stage = get(m, "stage")
            n_k = PAIR * H * QKHD
            nc.sync.dma_start(
                out=k_view[b][:, j0 : j0 + PAIR, :], in_=stage[:, 0:n_k].rearrange("p (j c) -> p j c", j=PAIR)
            )
            nc.sync.dma_start(
                out=v_view[b][:, j0 : j0 + PAIR, :],
                in_=stage[:, n_k : n_k + PAIR * N_V].rearrange("p (j c) -> p j c", j=PAIR),
            )

        def live(m):
            return 0 <= m < N_PAIRS

        for it in range(N_PAIRS + 6):
            if it >= N_PAIRS and live(it - 4):
                norm(it - 4)
            if live(it - 5):
                quant_z(it - 5)
            if live(it - 2):
                quant_x(it - 2)
            if it == 2:
                quantize(w2_q[:], w2_s[:], w2_g[:])
            if live(it - 1):
                turn_x(it - 1)
            if live(it - 5):
                second_product(it - 5)
            if live(it - 3):
                squares(it - 3)
                stats(it - 3)
            if it < N_PAIRS and live(it - 4):
                norm(it - 4)
            if live(it - 5):
                for i in range(PAIR):
                    out_bias(it - 5, i)
                rotate(it - 5)
                store(it - 5)
            if live(it):
                widen(it)
            if it == 0:
                prep_first_weights()
            if it == 1:
                prep_small()
                prep_second_weights()
            if live(it - 4):
                turn_z(it - 4)
            if live(it - 1):
                scale_x(it - 1)
            if live(it - 4):
                gain(it - 4)
            if live(it - 2):
                first_product(it - 2)
                for i in range(PAIR):
                    latent(it - 2, i)
                rope_bias(it - 2)
            if live(it - 4):
                interleave(it - 4)
